import numpy as np
import ml_dtypes


def mxq(x, axis, fmt="e4m3"):
    dtype, down = {"e4m3": (ml_dtypes.float8_e4m3fn, 7), "e5m2": (ml_dtypes.float8_e5m2, 14)}[fmt]
    v = np.moveaxis(np.asarray(x, np.float32).astype(ml_dtypes.bfloat16).astype(np.float64), axis, -1)
    blocks = v.reshape(v.shape[:-1] + (-1, 32))
    amax = np.abs(blocks).max(-1, keepdims=True)
    byte = np.maximum(np.where(amax > 0, np.frexp(amax)[1] - 1 + 127, 0) - down, 1)
    scale = np.exp2(byte - 127.0)
    codes = (blocks / scale).astype(np.float32).astype(dtype).astype(np.float64)
    return np.moveaxis((codes * scale).reshape(v.shape), -1, axis)


WIDE = False


def mx_kscale(k):
    if not WIDE:
        return np.ones(k)
    levels = np.array([10, -10, 5, -5, 0])
    a = np.random.permutation(np.resize(levels, k // 512 * 4)).reshape(k // 512, 4)
    idx = np.arange(k)
    return np.exp2(a[idx // 512, idx % 128 // 32])


BF16 = ml_dtypes.bfloat16


def bf(x):
    return np.asarray(x, np.float32).astype(BF16)


def f64(x):
    return np.asarray(x).astype(np.float64)


B, D, C, NP, NS = 1024, 2048, 512, 512, 512
ALPHA_NEG = 1.0 / 10.0


def relu(v):
    return np.maximum(v, 0.0)


def setup_inputs():
    t = mx_kscale(NP)
    u = mx_kscale(NS)
    return {
        "x_batch": bf(np.random.uniform(size=(B, D))),
        "predicted": bf(np.random.standard_normal((B, D))),
        "r_som": bf(np.maximum(np.random.standard_normal((B, NS)), 0.0) * 1.1 * u),
        "r_neg_batch": bf(np.random.uniform(size=(B, D)) * 0.5),
        "W_pv1_ff": bf(np.random.standard_normal((NP, D)) * 1.5 / np.sqrt(D) * t[:, None]),
        "W_inh_pe_neg": bf(np.random.standard_normal((D, NP)) * 1.2 / np.sqrt(NP) / t),
        "W_som_dend": bf(np.random.standard_normal((D, NS)) * 0.9 / np.sqrt(NS) / u),
    }


def reference(x_batch, predicted, r_som, r_neg_batch, W_pv1_ff, W_inh_pe_neg, W_som_dend):
    xf, pf = f64(x_batch), f64(predicted)
    r_pv1 = relu(mxq(xf, 1, "e4m3") @ mxq(f64(W_pv1_ff), 1, "e4m3").T)
    inh_pv = mxq(r_pv1, 1, "e4m3") @ mxq(f64(W_inh_pe_neg), 1, "e4m3").T
    inh_som = mxq(f64(r_som), 1, "e4m3") @ mxq(f64(W_som_dend), 1, "e4m3").T
    pe_neg = relu(pf - xf - inh_pv - inh_som)
    return (1.0 - ALPHA_NEG) * f64(r_neg_batch) + ALPHA_NEG * pe_neg

@@ -1,0 +1,199 @@
+from contextlib import ExitStack
+
+import concourse.mybir as mybir
+from concourse.masks import make_identity
+
+F32 = mybir.dt.float32
+BF16 = mybir.dt.bfloat16
+U32 = mybir.dt.uint32
+U8 = mybir.dt.uint8
+FP8X4 = mybir.dt.float8_e4m3fn_x4
+ALU = mybir.AluOpType
+ACT = mybir.ActivationFunctionType
+
+P = 128
+BATCH = 1024
+D = 2048
+NP = 512
+TILES = BATCH // P
+PAIR = 2
+UNIT = 2048
+WORDS = UNIT // 4
+CHUNK = 512
+CHUNKS = D // CHUNK
+HALF = D // 2
+
+FLOPS = 2 * BATCH * D * NP * 3
+
+
+def quantise_unit(nc, psum, stage, ident, src, codes, scales):
+    words = src.bitcast(F32)
+    grouped = stage.tile([P, UNIT], BF16, align_bytes=64)
+    grouped_words = grouped[:].bitcast(F32).rearrange("p (a r h) -> p a r h", a=4, h=2)
+    for half in range(2):
+        bank = psum.tile([P, 2, 2, P], F32, tag="bank")
+        for a in range(2):
+            for h in range(2):
+                first = (4 * half + 2 * a + h) * P
+                nc.tensor.transpose(bank[:, a, h, :], words[:, first : first + P], ident[:])
+        nc.scalar.copy(
+            out=grouped_words[:, 2 * half : 2 * half + 2, :, :],
+            in_=bank[:].rearrange("p a h r -> p a r h"),
+        )
+    nc.vector.quantize_mx(out=codes.bitcast(FP8X4), scales=scales, in_=grouped[:])
+
+
+def tile_pecircuits_pb_kernel(
+    tc, x_batch, predicted, r_som, r_neg_batch, W_pv1_ff, W_inh_pe_neg, W_som_dend, out
+):
+    nc = tc.nc
+    with ExitStack() as ctx:
+        const = ctx.enter_context(tc.tile_pool(name="const", bufs=1))
+        loads = ctx.enter_context(tc.tile_pool(name="loads", bufs=10))
+        keep = ctx.enter_context(tc.tile_pool(name="keep", bufs=1))
+        stage = ctx.enter_context(tc.tile_pool(name="stage", bufs=4))
+        psum = ctx.enter_context(tc.psum_pool(name="psum", bufs=8))
+
+        ident = const.tile([P, P], F32)
+        make_identity(nc, ident[:])
+
+        x_rows = x_batch.rearrange("(p j) d -> p j d", j=TILES)
+        pred_rows = predicted.rearrange("(p j) d -> p j d", j=TILES)
+        rneg_rows = r_neg_batch.rearrange("(p j) d -> p j d", j=TILES)
+        out_rows = out.rearrange("(p j) d -> p j d", j=TILES)
+
+        def load(view):
+            raw = loads.tile([P, 2 * UNIT], BF16, tag="raw", name="raw")
+            nc.sync.dma_start(out=raw[:].rearrange("p (a b) -> p a b", a=view.shape[1]), in_=view)
+            return raw
+
+        x_raw, pred_raw, rneg_raw = [], [], []
+        for q in range(TILES // PAIR):
+            x_raw.append(load(x_rows[:, PAIR * q : PAIR * q + PAIR, :]))
+            pred_raw.append(load(pred_rows[:, PAIR * q : PAIR * q + PAIR, :]))
+        w1_rows = W_pv1_ff.rearrange("(u p e) k -> u p e k", u=2, e=2)
+        w1_raw = [load(w1_rows[u]) for u in range(2)]
+        som_raw = load(r_som.rearrange("(p j) k -> p j k", j=TILES))
+        w2_rows = W_inh_pe_neg.rearrange("(c p t) k -> p c (t k)", c=CHUNKS, t=4)
+        w3_rows = W_som_dend.rearrange("(c p t) k -> p c (t k)", c=CHUNKS, t=4)
+        w2_raw, w3_raw = [], []
+        for q in range(CHUNKS // 2):
+            w2_raw.append(load(w2_rows[:, 2 * q : 2 * q + 2, :]))
+            w3_raw.append(load(w3_rows[:, 2 * q : 2 * q + 2, :]))
+        for q in range(TILES // PAIR):
+            rneg_raw.append(load(rneg_rows[:, PAIR * q : PAIR * q + PAIR, :]))
+
+        def half_of(raw, i):
+            return raw[:, i * UNIT : (i + 1) * UNIT]
+
+        def mx_tiles(units, name):
+            codes = keep.tile([P, units, WORDS], U32, align_bytes=64, name=name + "_codes")
+            scales = keep.tile([P, units, WORDS], U8, align_bytes=64, name=name + "_scales")
+            return codes, scales
+
+        x_codes, x_scales = mx_tiles(TILES, "x")
+        w1_codes, w1_scales = mx_tiles(4, "w1")
+        w2_codes, w2_scales = mx_tiles(CHUNKS, "w2")
+        w3_codes, w3_scales = mx_tiles(CHUNKS, "w3")
+        som_codes, som_scales = mx_tiles(2, "som")
+        r_codes, r_scales = mx_tiles(2, "r")
+
+        acc = []
+        for j in range(TILES):
+            x_tile = half_of(x_raw[j // PAIR], j % PAIR)
+            quantise_unit(nc, psum, stage, ident, x_tile, x_codes[:, j, :], x_scales[:, j, :])
+            acc_j = keep.tile([P, D], F32, name="acc%d" % j)
+            nc.vector.tensor_tensor(
+                out=acc_j[:], in0=half_of(pred_raw[j // PAIR], j % PAIR), in1=x_tile, op=ALU.subtract
+            )
+            acc.append(acc_j)
+
+        for t in range(4):
+            quantise_unit(
+                nc, psum, stage, ident, half_of(w1_raw[t // 2], t % 2), w1_codes[:, t, :], w1_scales[:, t, :]
+            )
+        for i in range(2):
+            quantise_unit(nc, psum, stage, ident, half_of(som_raw, i), som_codes[:, i, :], som_scales[:, i, :])
+        for c in range(CHUNKS):
+            quantise_unit(
+                nc, psum, stage, ident, half_of(w2_raw[c // 2], c % 2), w2_codes[:, c, :], w2_scales[:, c, :]
+            )
+            quantise_unit(
+                nc, psum, stage, ident, half_of(w3_raw[c // 2], c % 2), w3_codes[:, c, :], w3_scales[:, c, :]
+            )
+
+        def tile_cols(j):
+            return (j // 4, slice((j % 4) * P, (j % 4 + 1) * P))
+
+        for j in range(TILES):
+            unit, cols = tile_cols(j)
+            first = psum.tile([P, 4, P], F32, tag="bank")
+            for t in range(4):
+                for g in range(4):
+                    k_cols = slice(g * P, (g + 1) * P)
+                    nc.tensor.matmul_mx(
+                        out=first[:, t, :],
+                        lhsT=w1_codes[:, t, k_cols].bitcast(FP8X4),
+                        lhsT_scale=w1_scales[:, t, k_cols],
+                        rhs=x_codes[:, j, k_cols].bitcast(FP8X4),
+                        rhs_scale=x_scales[:, j, k_cols],
+                        start=(g == 0),
+                        stop=(g == 3),
+                    )
+            rates = stage.tile([P, P, 4], BF16, align_bytes=64)
+            nc.scalar.activation(out=rates[:], in_=first[:].rearrange("p t r -> p r t"), func=ACT.Relu)
+            nc.vector.quantize_mx(
+                out=r_codes[:, unit, cols].bitcast(FP8X4),
+                scales=r_scales[:, unit, cols],
+                in_=rates[:].rearrange("p r t -> p (r t)"),
+            )
+
+        def half_view(tile_ap, i):
+            return tile_ap[:, (i % 2) * HALF : (i % 2 + 1) * HALF]
+
+        def inhibit(i):
+            j = i // 2
+            unit, cols = tile_cols(j)
+            for c in range(2 * (i % 2), 2 * (i % 2) + 2):
+                inh = psum.tile([P, CHUNK], F32, tag="bank")
+                nc.tensor.matmul_mx(
+                    out=inh[:],
+                    lhsT=r_codes[:, unit, cols].bitcast(FP8X4),
+                    lhsT_scale=r_scales[:, unit, cols],
+                    rhs=w2_codes[:, c, :].bitcast(FP8X4),
+                    rhs_scale=w2_scales[:, c, :],
+                    start=True,
+                    stop=False,
+                )
+                nc.tensor.matmul_mx(
+                    out=inh[:],
+                    lhsT=som_codes[:, unit, cols].bitcast(FP8X4),
+                    lhsT_scale=som_scales[:, unit, cols],
+                    rhs=w3_codes[:, c, :].bitcast(FP8X4),
+                    rhs_scale=w3_scales[:, c, :],
+                    start=False,
+                    stop=True,
+                )
+                piece = acc[j][:, c * CHUNK : (c + 1) * CHUNK].rearrange("p (r t) -> p r t", t=4)
+                nc.vector.tensor_tensor(
+                    out=piece, in0=piece, in1=inh[:].rearrange("p (t r) -> p r t", t=4), op=ALU.subtract
+                )
+            nc.scalar.activation(out=half_view(acc[j], i), in_=half_view(acc[j], i), func=ACT.Relu, scale=0.1)
+
+        def filter_and_store(i):
+            j = i // 2
+            nc.vector.scalar_tensor_tensor(
+                out=half_view(acc[j], i),
+                in0=half_view(half_of(rneg_raw[j // PAIR], j % PAIR), i),
+                scalar=0.9,
+                in1=half_view(acc[j], i),
+                op0=ALU.mult,
+                op1=ALU.add,
+            )
+            nc.sync.dma_start(out=half_view(out_rows[:, j, :], i), in_=half_view(acc[j], i))
+
+        for i in range(2 * TILES):
+            inhibit(i)
+            if i > 0:
+                filter_and_store(i - 1)
+        filter_and_store(2 * TILES - 1)

@@ -17,6 +17,7 @@ D = 2048
 NP = 512
 TILES = BATCH // P
 PAIR = 2
+GROUP = 4
 UNIT = 2048
 WORDS = UNIT // 4
 CHUNK = 512
@@ -25,23 +26,8 @@ HALF = D // 2
 
 FLOPS = 2 * BATCH * D * NP * 3
 
-
-def quantise_unit(nc, psum, stage, ident, src, codes, scales):
-    words = src.bitcast(F32)
-    grouped = stage.tile([P, UNIT], BF16, align_bytes=64)
-    grouped_words = grouped[:].bitcast(F32).rearrange("p (a r h) -> p a r h", a=4, h=2)
-    for half in range(2):
-        bank = psum.tile([P, 2, 2, P], F32, tag="bank")
-        for a in range(2):
-            for h in range(2):
-                first = (4 * half + 2 * a + h) * P
-                nc.tensor.transpose(bank[:, a, h, :], words[:, first : first + P], ident[:])
-        nc.scalar.copy(
-            out=grouped_words[:, 2 * half : 2 * half + 2, :, :],
-            in_=bank[:].rearrange("p a h r -> p a r h"),
-        )
-    nc.vector.quantize_mx(out=codes.bitcast(FP8X4), scales=scales, in_=grouped[:])
-
+LEAD = 2
+AHEAD = 2
 
 def tile_pecircuits_pb_kernel(
     tc, x_batch, predicted, r_som, r_neg_batch, W_pv1_ff, W_inh_pe_neg, W_som_dend, out
@@ -52,148 +38,213 @@ def tile_pecircuits_pb_kernel(
         loads = ctx.enter_context(tc.tile_pool(name="loads", bufs=10))
         keep = ctx.enter_context(tc.tile_pool(name="keep", bufs=1))
         stage = ctx.enter_context(tc.tile_pool(name="stage", bufs=4))
-        psum = ctx.enter_context(tc.psum_pool(name="psum", bufs=8))
+        psum_prep = ctx.enter_context(tc.psum_pool(name="psum_prep", bufs=4))
+        psum_inh = ctx.enter_context(tc.psum_pool(name="psum_inh", bufs=4))
+        ctx.enter_context(tc.manual_schedule())
 
         ident = const.tile([P, P], F32)
         make_identity(nc, ident[:])
+        plus = const.tile([P, P], BF16)
+        make_identity(nc, plus[:])
+        minus = const.tile([P, P], BF16)
+        nc.gpsimd.tensor_scalar_mul(out=minus[:], in0=plus[:], scalar1=-1.0)
 
-        x_rows = x_batch.rearrange("(p j) d -> p j d", j=TILES)
-        pred_rows = predicted.rearrange("(p j) d -> p j d", j=TILES)
-        rneg_rows = r_neg_batch.rearrange("(p j) d -> p j d", j=TILES)
-        out_rows = out.rearrange("(p j) d -> p j d", j=TILES)
-
-        def load(view):
+        def load(*views):
             raw = loads.tile([P, 2 * UNIT], BF16, tag="raw", name="raw")
-            nc.sync.dma_start(out=raw[:].rearrange("p (a b) -> p a b", a=view.shape[1]), in_=view)
+            width = 2 * UNIT // len(views)
+            for i, view in enumerate(views):
+                nc.sync.dma_start(out=raw[:, i * width : (i + 1) * width], in_=view)
             return raw
-
-        x_raw, pred_raw, rneg_raw = [], [], []
-        for q in range(TILES // PAIR):
-            x_raw.append(load(x_rows[:, PAIR * q : PAIR * q + PAIR, :]))
-            pred_raw.append(load(pred_rows[:, PAIR * q : PAIR * q + PAIR, :]))
-        w1_rows = W_pv1_ff.rearrange("(u p e) k -> u p e k", u=2, e=2)
-        w1_raw = [load(w1_rows[u]) for u in range(2)]
-        som_raw = load(r_som.rearrange("(p j) k -> p j k", j=TILES))
-        w2_rows = W_inh_pe_neg.rearrange("(c p t) k -> p c (t k)", c=CHUNKS, t=4)
-        w3_rows = W_som_dend.rearrange("(c p t) k -> p c (t k)", c=CHUNKS, t=4)
-        w2_raw, w3_raw = [], []
-        for q in range(CHUNKS // 2):
-            w2_raw.append(load(w2_rows[:, 2 * q : 2 * q + 2, :]))
-            w3_raw.append(load(w3_rows[:, 2 * q : 2 * q + 2, :]))
-        for q in range(TILES // PAIR):
-            rneg_raw.append(load(rneg_rows[:, PAIR * q : PAIR * q + PAIR, :]))
 
         def half_of(raw, i):
             return raw[:, i * UNIT : (i + 1) * UNIT]
+
+        x_rows = x_batch.rearrange("(p j) d -> p (j d)", j=TILES)
+        pred_rows = predicted.rearrange("(p j) d -> p (j d)", j=TILES)
+        rneg_rows = r_neg_batch.rearrange("(p j) d -> p (j d)", j=TILES)
+        out_rows = out.rearrange("(p j) d -> p j d", j=TILES)
+        w1_rows = W_pv1_ff.rearrange("(u p e) k -> u p (e k)", u=2, e=2)
+        w2_rows = W_inh_pe_neg.rearrange("(c p t) k -> c p (t k)", c=CHUNKS, t=4)
+        w3_rows = W_som_dend.rearrange("(c p t) k -> c p (t k)", c=CHUNKS, t=4)
+
+        def pair_of(rows, q):
+            return rows[:, q * PAIR * D : (q + 1) * PAIR * D]
+
+        x_raw = [load(pair_of(x_rows, 0))]
+        pred_raw = [load(pair_of(pred_rows, 0))]
+        w1_raw = [load(w1_rows[u]) for u in range(2)]
+        x_raw.append(load(pair_of(x_rows, 1)))
+        pred_raw.append(load(pair_of(pred_rows, 1)))
+        som_raw = load(r_som.rearrange("(p j) k -> p (j k)", j=TILES))
+        w23_raw = [load(w2_rows[c], w3_rows[c]) for c in range(CHUNKS)]
+        rneg_raw = [load(pair_of(rneg_rows, q)) for q in range(2)]
+        for q in range(2, TILES // PAIR):
+            x_raw.append(load(pair_of(x_rows, q)))
+            pred_raw.append(load(pair_of(pred_rows, q)))
+        for q in range(2, TILES // PAIR):
+            rneg_raw.append(load(pair_of(rneg_rows, q)))
 
         def mx_tiles(units, name):
             codes = keep.tile([P, units, WORDS], U32, align_bytes=64, name=name + "_codes")
             scales = keep.tile([P, units, WORDS], U8, align_bytes=64, name=name + "_scales")
             return codes, scales
 
-        x_codes, x_scales = mx_tiles(TILES, "x")
-        w1_codes, w1_scales = mx_tiles(4, "w1")
-        w2_codes, w2_scales = mx_tiles(CHUNKS, "w2")
-        w3_codes, w3_scales = mx_tiles(CHUNKS, "w3")
-        som_codes, som_scales = mx_tiles(2, "som")
-        r_codes, r_scales = mx_tiles(2, "r")
+        x_mx = mx_tiles(TILES, "x")
+        w1_mx = mx_tiles(4, "w1")
+        w2_mx = mx_tiles(CHUNKS, "w2")
+        w3_mx = mx_tiles(CHUNKS, "w3")
+        som_mx = mx_tiles(2, "som")
+        r_mx = mx_tiles(2, "r")
+        acc = [keep.tile([P, D], F32, name="acc%d" % j) for j in range(TILES)]
 
-        acc = []
-        for j in range(TILES):
-            x_tile = half_of(x_raw[j // PAIR], j % PAIR)
-            quantise_unit(nc, psum, stage, ident, x_tile, x_codes[:, j, :], x_scales[:, j, :])
-            acc_j = keep.tile([P, D], F32, name="acc%d" % j)
-            nc.vector.tensor_tensor(
-                out=acc_j[:], in0=half_of(pred_raw[j // PAIR], j % PAIR), in1=x_tile, op=ALU.subtract
-            )
-            acc.append(acc_j)
+        def transpose_unit(src):
+            words = src.bitcast(F32)
+            grouped = stage.tile([P, UNIT], BF16, align_bytes=64)
+            grouped_words = grouped[:].bitcast(F32).rearrange("p (a r h) -> p a r h", a=4, h=2)
+            for half in range(2):
+                bank = psum_prep.tile([P, 2, 2, P], F32, tag="prep")
+                for a in range(2):
+                    for h in range(2):
+                        start = (4 * half + 2 * a + h) * P
+                        nc.tensor.transpose(bank[:, a, h, :], words[:, start : start + P], ident[:])
+                nc.scalar.copy(
+                    out=grouped_words[:, 2 * half : 2 * half + 2, :, :],
+                    in_=bank[:].rearrange("p a h r -> p a r h"),
+                )
+            return grouped
 
-        for t in range(4):
-            quantise_unit(
-                nc, psum, stage, ident, half_of(w1_raw[t // 2], t % 2), w1_codes[:, t, :], w1_scales[:, t, :]
-            )
-        for i in range(2):
-            quantise_unit(nc, psum, stage, ident, half_of(som_raw, i), som_codes[:, i, :], som_scales[:, i, :])
-        for c in range(CHUNKS):
-            quantise_unit(
-                nc, psum, stage, ident, half_of(w2_raw[c // 2], c % 2), w2_codes[:, c, :], w2_scales[:, c, :]
-            )
-            quantise_unit(
-                nc, psum, stage, ident, half_of(w3_raw[c // 2], c % 2), w3_codes[:, c, :], w3_scales[:, c, :]
-            )
+        def quantise(grouped, mx, unit):
+            nc.vector.quantize_mx(out=mx[0][:, unit, :].bitcast(FP8X4), scales=mx[1][:, unit, :], in_=grouped[:])
 
-        def tile_cols(j):
-            return (j // 4, slice((j % 4) * P, (j % 4 + 1) * P))
+        def x_tile(j):
+            return half_of(x_raw[j // PAIR], j % PAIR)
 
-        for j in range(TILES):
-            unit, cols = tile_cols(j)
-            first = psum.tile([P, 4, P], F32, tag="bank")
+        def pred_tile(j):
+            return half_of(pred_raw[j // PAIR], j % PAIR)
+
+        def difference_on_vector(j):
+            nc.vector.tensor_tensor(out=acc[j][:], in0=pred_tile(j), in1=x_tile(j), op=ALU.subtract)
+
+        def difference_on_tensor(j, h):
+            for c in range(2 * h, 2 * h + 2):
+                cols = slice(c * CHUNK, (c + 1) * CHUNK)
+                diff = psum_prep.tile([P, CHUNK], F32, tag="prep")
+                nc.tensor.matmul(out=diff[:], lhsT=plus[:], rhs=pred_tile(j)[:, cols], start=True, stop=False)
+                nc.tensor.matmul(out=diff[:], lhsT=minus[:], rhs=x_tile(j)[:, cols], start=False, stop=True)
+                nc.scalar.copy(out=acc[j][:, cols], in_=diff[:])
+
+        def operand(mx, unit, cols):
+            return mx[0][:, unit, cols].bitcast(FP8X4), mx[1][:, unit, cols]
+
+        def batch_operand(mx, j):
+            return operand(mx, j // 4, slice((j % 4) * P, (j % 4 + 1) * P))
+
+        def first_product(j):
+            first = psum_prep.tile([P, 4, P], F32, tag="prep")
             for t in range(4):
                 for g in range(4):
                     k_cols = slice(g * P, (g + 1) * P)
+                    w_codes, w_scales = operand(w1_mx, t, k_cols)
+                    b_codes, b_scales = operand(x_mx, j, k_cols)
                     nc.tensor.matmul_mx(
-                        out=first[:, t, :],
-                        lhsT=w1_codes[:, t, k_cols].bitcast(FP8X4),
-                        lhsT_scale=w1_scales[:, t, k_cols],
-                        rhs=x_codes[:, j, k_cols].bitcast(FP8X4),
-                        rhs_scale=x_scales[:, j, k_cols],
-                        start=(g == 0),
-                        stop=(g == 3),
+                        out=first[:, t, :], lhsT=w_codes, lhsT_scale=w_scales, rhs=b_codes, rhs_scale=b_scales,
+                        start=(g == 0), stop=(g == 3),
                     )
             rates = stage.tile([P, P, 4], BF16, align_bytes=64)
             nc.scalar.activation(out=rates[:], in_=first[:].rearrange("p t r -> p r t"), func=ACT.Relu)
-            nc.vector.quantize_mx(
-                out=r_codes[:, unit, cols].bitcast(FP8X4),
-                scales=r_scales[:, unit, cols],
-                in_=rates[:].rearrange("p r t -> p (r t)"),
-            )
+            return rates
 
-        def half_view(tile_ap, i):
-            return tile_ap[:, (i % 2) * HALF : (i % 2 + 1) * HALF]
+        def quantise_rates(rates, j):
+            codes, scales = batch_operand(r_mx, j)
+            nc.vector.quantize_mx(out=codes, scales=scales, in_=rates[:].rearrange("p r t -> p (r t)"))
 
-        def inhibit(i):
-            j = i // 2
-            unit, cols = tile_cols(j)
-            for c in range(2 * (i % 2), 2 * (i % 2) + 2):
-                inh = psum.tile([P, CHUNK], F32, tag="bank")
+        def half_view(tile_ap, h):
+            return tile_ap[:, h * HALF : (h + 1) * HALF]
+
+        def products(j, h):
+            r_codes, r_scales = batch_operand(r_mx, j)
+            s_codes, s_scales = batch_operand(som_mx, j)
+            banks = []
+            for c in range(2 * h, 2 * h + 2):
+                w2_codes, w2_scales = operand(w2_mx, c, slice(0, WORDS))
+                w3_codes, w3_scales = operand(w3_mx, c, slice(0, WORDS))
+                inh = psum_inh.tile([P, CHUNK], F32)
                 nc.tensor.matmul_mx(
-                    out=inh[:],
-                    lhsT=r_codes[:, unit, cols].bitcast(FP8X4),
-                    lhsT_scale=r_scales[:, unit, cols],
-                    rhs=w2_codes[:, c, :].bitcast(FP8X4),
-                    rhs_scale=w2_scales[:, c, :],
-                    start=True,
-                    stop=False,
+                    out=inh[:], lhsT=r_codes, lhsT_scale=r_scales, rhs=w2_codes, rhs_scale=w2_scales,
+                    start=True, stop=False,
                 )
                 nc.tensor.matmul_mx(
-                    out=inh[:],
-                    lhsT=som_codes[:, unit, cols].bitcast(FP8X4),
-                    lhsT_scale=som_scales[:, unit, cols],
-                    rhs=w3_codes[:, c, :].bitcast(FP8X4),
-                    rhs_scale=w3_scales[:, c, :],
-                    start=False,
-                    stop=True,
+                    out=inh[:], lhsT=s_codes, lhsT_scale=s_scales, rhs=w3_codes, rhs_scale=w3_scales,
+                    start=False, stop=True,
                 )
+                banks.append(inh)
+            return banks
+
+        def subtract_and_relu(j, h, banks):
+            for i in range(2):
+                c = 2 * h + i
                 piece = acc[j][:, c * CHUNK : (c + 1) * CHUNK].rearrange("p (r t) -> p r t", t=4)
                 nc.vector.tensor_tensor(
-                    out=piece, in0=piece, in1=inh[:].rearrange("p (t r) -> p r t", t=4), op=ALU.subtract
+                    out=piece, in0=piece, in1=banks[i][:].rearrange("p (t r) -> p r t", t=4), op=ALU.subtract
                 )
-            nc.scalar.activation(out=half_view(acc[j], i), in_=half_view(acc[j], i), func=ACT.Relu, scale=0.1)
+            nc.scalar.activation(out=half_view(acc[j], h), in_=half_view(acc[j], h), func=ACT.Relu, scale=0.1)
 
-        def filter_and_store(i):
-            j = i // 2
+        def filter_and_store(j, h):
             nc.vector.scalar_tensor_tensor(
-                out=half_view(acc[j], i),
-                in0=half_view(half_of(rneg_raw[j // PAIR], j % PAIR), i),
+                out=half_view(acc[j], h),
+                in0=half_view(half_of(rneg_raw[j // PAIR], j % PAIR), h),
                 scalar=0.9,
-                in1=half_view(acc[j], i),
+                in1=half_view(acc[j], h),
                 op0=ALU.mult,
                 op1=ALU.add,
             )
-            nc.sync.dma_start(out=half_view(out_rows[:, j, :], i), in_=half_view(acc[j], i))
+            nc.sync.dma_start(out=half_view(out_rows[:, j, :], h), in_=half_view(acc[j], h))
 
-        for i in range(2 * TILES):
-            inhibit(i)
-            if i > 0:
-                filter_and_store(i - 1)
-        filter_and_store(2 * TILES - 1)
+        rates = {}
+        grouped = {}
+        for j in range(PAIR):
+            quantise(transpose_unit(x_tile(j)), x_mx, j)
+            difference_on_vector(j)
+        for t in range(4):
+            quantise(transpose_unit(half_of(w1_raw[t // 2], t % 2)), w1_mx, t)
+        for j in range(PAIR, GROUP):
+            grouped[j] = transpose_unit(x_tile(j))
+        for j in range(PAIR):
+            rates[j] = first_product(j)
+        for j in range(PAIR, GROUP):
+            quantise(grouped[j], x_mx, j)
+            difference_on_vector(j)
+        for i in range(2):
+            grouped[i] = transpose_unit(half_of(som_raw, i))
+        for j in range(PAIR, GROUP):
+            rates[j] = first_product(j)
+        for i in range(2):
+            quantise(grouped[i], som_mx, i)
+        for j in range(GROUP):
+            quantise_rates(rates[j], j)
+        for c in range(2):
+            quantise(transpose_unit(half_of(w23_raw[c], 0)), w2_mx, c)
+            quantise(transpose_unit(half_of(w23_raw[c], 1)), w3_mx, c)
+
+        late = [(half_of(w23_raw[c], i), (w2_mx, w3_mx)[i], c) for c in range(2, CHUNKS) for i in range(2)]
+        late.extend([(x_tile(j), x_mx, j) for j in range(GROUP, TILES)])
+        steps = [(j, h) for g in range(TILES // GROUP) for h in range(2) for j in range(GROUP * g, GROUP * (g + 1))]
+        banks = {}
+        for s in range(-LEAD, len(steps) + 1):
+            if 0 <= s + 1 < len(steps):
+                banks[s + 1] = products(steps[s + 1][0], steps[s + 1][1])
+            if 0 <= s < len(steps):
+                subtract_and_relu(steps[s][0], steps[s][1], banks[s])
+            if s >= 1:
+                filter_and_store(steps[s - 1][0], steps[s - 1][1])
+            u = s + LEAD
+            if u < len(late):
+                grouped[u] = transpose_unit(late[u][0])
+            if 0 <= u - 1 < len(late):
+                quantise(grouped[u - 1], late[u - 1][1], late[u - 1][2])
+                if late[u - 1][1] is x_mx:
+                    rates[late[u - 1][2]] = first_product(late[u - 1][2])
+            if 0 <= u - 2 < len(late) and late[u - 2][1] is x_mx:
+                quantise_rates(rates[late[u - 2][2]], late[u - 2][2])
+            if 0 <= s + AHEAD < len(steps) and steps[s + AHEAD][0] >= GROUP:
+                difference_on_tensor(steps[s + AHEAD][0], steps[s + AHEAD][1])

@@ -26,8 +26,11 @@ HALF = D // 2
 
 FLOPS = 2 * BATCH * D * NP * 3
 
-LEAD = 2
-AHEAD = 2
+SLOTS = 4
+RES = 6
+LDS = 13
+LAG = 2
+
 
 def tile_pecircuits_pb_kernel(
     tc, x_batch, predicted, r_som, r_neg_batch, W_pv1_ff, W_inh_pe_neg, W_som_dend, out
@@ -35,9 +38,11 @@ def tile_pecircuits_pb_kernel(
     nc = tc.nc
     with ExitStack() as ctx:
         const = ctx.enter_context(tc.tile_pool(name="const", bufs=1))
-        loads = ctx.enter_context(tc.tile_pool(name="loads", bufs=10))
+        loads = ctx.enter_context(tc.tile_pool(name="loads", bufs=LDS))
         keep = ctx.enter_context(tc.tile_pool(name="keep", bufs=1))
         stage = ctx.enter_context(tc.tile_pool(name="stage", bufs=4))
+        errors = ctx.enter_context(tc.tile_pool(name="errors", bufs=SLOTS))
+        results = ctx.enter_context(tc.tile_pool(name="results", bufs=RES))
         psum_prep = ctx.enter_context(tc.psum_pool(name="psum_prep", bufs=4))
         psum_inh = ctx.enter_context(tc.psum_pool(name="psum_inh", bufs=4))
         ctx.enter_context(tc.manual_schedule())
@@ -70,19 +75,29 @@ def tile_pecircuits_pb_kernel(
         def pair_of(rows, q):
             return rows[:, q * PAIR * D : (q + 1) * PAIR * D]
 
-        x_raw = [load(pair_of(x_rows, 0))]
-        pred_raw = [load(pair_of(pred_rows, 0))]
+        def tile_of(rows, j):
+            return rows[:, j * D : (j + 1) * D]
+
+        x_raw, pred_raw, rneg_raw, w23_raw = {}, {}, {}, {}
+        x_raw[0] = load(tile_of(x_rows, 0), tile_of(x_rows, 1))
         w1_raw = [load(w1_rows[u]) for u in range(2)]
-        x_raw.append(load(pair_of(x_rows, 1)))
-        pred_raw.append(load(pair_of(pred_rows, 1)))
-        som_raw = load(r_som.rearrange("(p j) k -> p (j k)", j=TILES))
-        w23_raw = [load(w2_rows[c], w3_rows[c]) for c in range(CHUNKS)]
-        rneg_raw = [load(pair_of(rneg_rows, q)) for q in range(2)]
-        for q in range(2, TILES // PAIR):
-            x_raw.append(load(pair_of(x_rows, q)))
-            pred_raw.append(load(pair_of(pred_rows, q)))
-        for q in range(2, TILES // PAIR):
-            rneg_raw.append(load(pair_of(rneg_rows, q)))
+        som_rows = r_som.rearrange("(p j) k -> p (j k)", j=TILES)
+        som_raw = loads.tile([P, 2 * UNIT], BF16, tag="raw", name="som_raw")
+        nc.sync.dma_start(out=half_of(som_raw, 0), in_=half_of(som_rows, 0))
+        w23_raw[0] = load(w2_rows[0], w3_rows[0])
+        pred_raw[0] = load(pair_of(pred_rows, 0))
+        for c in range(1, CHUNKS):
+            w23_raw[c] = load(w2_rows[c], w3_rows[c])
+        x_raw[1] = load(pair_of(x_rows, 1))
+        rneg_raw[0] = load(pair_of(rneg_rows, 0))
+        pred_raw[1] = load(pair_of(pred_rows, 1))
+        nc.sync.dma_start(out=half_of(som_raw, 1), in_=half_of(som_rows, 1))
+        pending = [(x_raw, x_rows, 2), (rneg_raw, rneg_rows, 1), (pred_raw, pred_rows, 2), (x_raw, x_rows, 3), (rneg_raw, rneg_rows, 2), (pred_raw, pred_rows, 3), (rneg_raw, rneg_rows, 3)]
+
+        def load_next():
+            if pending:
+                raws, rows, q = pending.pop(0)
+                raws[q] = load(pair_of(rows, q))
 
         def mx_tiles(units, name):
             codes = keep.tile([P, units, WORDS], U32, align_bytes=64, name=name + "_codes")
@@ -95,22 +110,25 @@ def tile_pecircuits_pb_kernel(
         w3_mx = mx_tiles(CHUNKS, "w3")
         som_mx = mx_tiles(2, "som")
         r_mx = mx_tiles(2, "r")
-        acc = [keep.tile([P, D], F32, name="acc%d" % j) for j in range(TILES)]
 
-        def transpose_unit(src):
+        def transpose_half(src, grouped, half, on_vector):
             words = src.bitcast(F32)
-            grouped = stage.tile([P, UNIT], BF16, align_bytes=64)
             grouped_words = grouped[:].bitcast(F32).rearrange("p (a r h) -> p a r h", a=4, h=2)
+            bank = psum_prep.tile([P, 2, 2, P], F32, tag="prep", name="bank")
+            for a in range(2):
+                for h in range(2):
+                    start = (4 * half + 2 * a + h) * P
+                    nc.tensor.transpose(bank[:, a, h, :], words[:, start : start + P], ident[:])
+            copy = nc.vector.tensor_copy if on_vector else nc.scalar.copy
+            copy(
+                out=grouped_words[:, 2 * half : 2 * half + 2, :, :],
+                in_=bank[:].rearrange("p a h r -> p a r h"),
+            )
+
+        def transpose_unit(src, shared=False):
+            grouped = stage.tile([P, UNIT], BF16, align_bytes=64, name="grouped")
             for half in range(2):
-                bank = psum_prep.tile([P, 2, 2, P], F32, tag="prep")
-                for a in range(2):
-                    for h in range(2):
-                        start = (4 * half + 2 * a + h) * P
-                        nc.tensor.transpose(bank[:, a, h, :], words[:, start : start + P], ident[:])
-                nc.scalar.copy(
-                    out=grouped_words[:, 2 * half : 2 * half + 2, :, :],
-                    in_=bank[:].rearrange("p a h r -> p a r h"),
-                )
+                transpose_half(src, grouped, half, shared and half == 1)
             return grouped
 
         def quantise(grouped, mx, unit):
@@ -122,26 +140,13 @@ def tile_pecircuits_pb_kernel(
         def pred_tile(j):
             return half_of(pred_raw[j // PAIR], j % PAIR)
 
-        def difference_on_vector(j):
-            nc.vector.tensor_tensor(out=acc[j][:], in0=pred_tile(j), in1=x_tile(j), op=ALU.subtract)
-
-        def difference_on_tensor(j, h):
-            for c in range(2 * h, 2 * h + 2):
-                cols = slice(c * CHUNK, (c + 1) * CHUNK)
-                diff = psum_prep.tile([P, CHUNK], F32, tag="prep")
-                nc.tensor.matmul(out=diff[:], lhsT=plus[:], rhs=pred_tile(j)[:, cols], start=True, stop=False)
-                nc.tensor.matmul(out=diff[:], lhsT=minus[:], rhs=x_tile(j)[:, cols], start=False, stop=True)
-                nc.scalar.copy(out=acc[j][:, cols], in_=diff[:])
-
         def operand(mx, unit, cols):
             return mx[0][:, unit, cols].bitcast(FP8X4), mx[1][:, unit, cols]
 
         def batch_operand(mx, j):
             return operand(mx, j // 4, slice((j % 4) * P, (j % 4 + 1) * P))
 
-        def first_product(j):
-            first = psum_prep.tile([P, 4, P], F32, tag="prep")
-            for t in range(4):
+        def first_part(first, j, t):
                 for g in range(4):
                     k_cols = slice(g * P, (g + 1) * P)
                     w_codes, w_scales = operand(w1_mx, t, k_cols)
@@ -150,25 +155,58 @@ def tile_pecircuits_pb_kernel(
                         out=first[:, t, :], lhsT=w_codes, lhsT_scale=w_scales, rhs=b_codes, rhs_scale=b_scales,
                         start=(g == 0), stop=(g == 3),
                     )
-            rates = stage.tile([P, P, 4], BF16, align_bytes=64)
+
+        def rates_of(first):
+            rates = stage.tile([P, P, 4], BF16, align_bytes=64, name="rates")
             nc.scalar.activation(out=rates[:], in_=first[:].rearrange("p t r -> p r t"), func=ACT.Relu)
             return rates
+
+        def first_product(j):
+            first = psum_prep.tile([P, 4, P], F32, tag="prep", name="first")
+            for t in range(4):
+                first_part(first, j, t)
+            return first
 
         def quantise_rates(rates, j):
             codes, scales = batch_operand(r_mx, j)
             nc.vector.quantize_mx(out=codes, scales=scales, in_=rates[:].rearrange("p r t -> p (r t)"))
 
-        def half_view(tile_ap, h):
-            return tile_ap[:, h * HALF : (h + 1) * HALF]
+        steps = [(j, h) for h in range(2) for j in range(PAIR)] + [(j, h) for j in range(PAIR, TILES) for h in range(2)]
+        banks = {}
+        errs = {}
 
-        def products(j, h):
+        def new_error(s):
+            errs[s] = errors.tile([P, HALF], F32, name="err")
+
+        def difference(s, i, engine):
+            j, h = steps[s]
+            cols = slice((2 * h + i) * CHUNK, (2 * h + i + 1) * CHUNK)
+            piece = errs[s][:, i * CHUNK : (i + 1) * CHUNK]
+            engine.tensor_tensor(out=piece, in0=pred_tile(j)[:, cols], in1=x_tile(j)[:, cols], op=ALU.subtract)
+
+        def difference_wide(s):
+            j, h = steps[s]
+            cols = slice(h * HALF, (h + 1) * HALF)
+            nc.vector.tensor_tensor(out=errs[s][:], in0=pred_tile(j)[:, cols], in1=x_tile(j)[:, cols], op=ALU.subtract)
+
+        def difference_on_tensor(s, i):
+            j, h = steps[s]
+            cols = slice((2 * h + i) * CHUNK, (2 * h + i + 1) * CHUNK)
+            piece = errs[s][:, i * CHUNK : (i + 1) * CHUNK]
+            diff = psum_prep.tile([P, CHUNK], F32, tag="prep", name="diff")
+            nc.tensor.matmul(out=diff[:], lhsT=plus[:], rhs=pred_tile(j)[:, cols], start=True, stop=False)
+            nc.tensor.matmul(out=diff[:], lhsT=minus[:], rhs=x_tile(j)[:, cols], start=False, stop=True)
+            nc.scalar.copy(out=piece, in_=diff[:])
+
+        def products(s, which=(0, 1)):
+            j, h = steps[s]
             r_codes, r_scales = batch_operand(r_mx, j)
             s_codes, s_scales = batch_operand(som_mx, j)
-            banks = []
-            for c in range(2 * h, 2 * h + 2):
+            banks.setdefault(s, [])
+            for c in (2 * h + i for i in which):
                 w2_codes, w2_scales = operand(w2_mx, c, slice(0, WORDS))
                 w3_codes, w3_scales = operand(w3_mx, c, slice(0, WORDS))
-                inh = psum_inh.tile([P, CHUNK], F32)
+                inh = psum_inh.tile([P, CHUNK], F32, tag="inh", name="inh")
                 nc.tensor.matmul_mx(
                     out=inh[:], lhsT=r_codes, lhsT_scale=r_scales, rhs=w2_codes, rhs_scale=w2_scales,
                     start=True, stop=False,
@@ -177,74 +215,148 @@ def tile_pecircuits_pb_kernel(
                     out=inh[:], lhsT=s_codes, lhsT_scale=s_scales, rhs=w3_codes, rhs_scale=w3_scales,
                     start=False, stop=True,
                 )
-                banks.append(inh)
-            return banks
+                banks[s].append(inh)
 
-        def subtract_and_relu(j, h, banks):
-            for i in range(2):
-                c = 2 * h + i
-                piece = acc[j][:, c * CHUNK : (c + 1) * CHUNK].rearrange("p (r t) -> p r t", t=4)
+        def subtract(s, which=(0, 1)):
+            for i in which:
+                piece = errs[s][:, i * CHUNK : (i + 1) * CHUNK].rearrange("p (r t) -> p r t", t=4)
                 nc.vector.tensor_tensor(
-                    out=piece, in0=piece, in1=banks[i][:].rearrange("p (t r) -> p r t", t=4), op=ALU.subtract
+                    out=piece, in0=piece, in1=banks[s][i][:].rearrange("p (t r) -> p r t", t=4), op=ALU.subtract
                 )
-            nc.scalar.activation(out=half_view(acc[j], h), in_=half_view(acc[j], h), func=ACT.Relu, scale=0.1)
 
-        def filter_and_store(j, h):
+        def relu(s):
+            nc.scalar.activation(out=errs[s][:], in_=errs[s][:], func=ACT.Relu, scale=0.1)
+
+        def filter_and_store(s):
+            j, h = steps[s]
+            cols = slice(h * HALF, (h + 1) * HALF)
+            res = results.tile([P, HALF], F32, name="res")
             nc.vector.scalar_tensor_tensor(
-                out=half_view(acc[j], h),
-                in0=half_view(half_of(rneg_raw[j // PAIR], j % PAIR), h),
-                scalar=0.9,
-                in1=half_view(acc[j], h),
-                op0=ALU.mult,
-                op1=ALU.add,
+                out=res[:], in0=half_of(rneg_raw[j // PAIR], j % PAIR)[:, cols], scalar=0.9, in1=errs[s][:],
+                op0=ALU.mult, op1=ALU.add,
             )
-            nc.sync.dma_start(out=half_view(out_rows[:, j, :], h), in_=half_view(acc[j], h))
+            nc.sync.dma_start(out=out_rows[:, j, cols], in_=res[:])
+
+        def unit_of(name, i):
+            if name == "x":
+                return x_tile(i), x_mx, i
+            if name == "w1":
+                return half_of(w1_raw[i // 2], i % 2), w1_mx, i
+            if name == "som":
+                return half_of(som_raw, i), som_mx, i
+            return half_of(w23_raw[i], 0 if name == "w2" else 1), (w2_mx if name == "w2" else w3_mx), i
 
         rates = {}
         grouped = {}
-        for j in range(PAIR):
-            quantise(transpose_unit(x_tile(j)), x_mx, j)
-            difference_on_vector(j)
-        for t in range(4):
-            quantise(transpose_unit(half_of(w1_raw[t // 2], t % 2)), w1_mx, t)
-        for j in range(PAIR, GROUP):
-            grouped[j] = transpose_unit(x_tile(j))
-        for j in range(PAIR):
-            rates[j] = first_product(j)
-        for j in range(PAIR, GROUP):
-            quantise(grouped[j], x_mx, j)
-            difference_on_vector(j)
-        for i in range(2):
-            grouped[i] = transpose_unit(half_of(som_raw, i))
-        for j in range(PAIR, GROUP):
-            rates[j] = first_product(j)
-        for i in range(2):
-            quantise(grouped[i], som_mx, i)
-        for j in range(GROUP):
-            quantise_rates(rates[j], j)
-        for c in range(2):
-            quantise(transpose_unit(half_of(w23_raw[c], 0)), w2_mx, c)
-            quantise(transpose_unit(half_of(w23_raw[c], 1)), w3_mx, c)
 
-        late = [(half_of(w23_raw[c], i), (w2_mx, w3_mx)[i], c) for c in range(2, CHUNKS) for i in range(2)]
-        late.extend([(x_tile(j), x_mx, j) for j in range(GROUP, TILES)])
-        steps = [(j, h) for g in range(TILES // GROUP) for h in range(2) for j in range(GROUP * g, GROUP * (g + 1))]
-        banks = {}
-        for s in range(-LEAD, len(steps) + 1):
-            if 0 <= s + 1 < len(steps):
-                banks[s + 1] = products(steps[s + 1][0], steps[s + 1][1])
-            if 0 <= s < len(steps):
-                subtract_and_relu(steps[s][0], steps[s][1], banks[s])
-            if s >= 1:
-                filter_and_store(steps[s - 1][0], steps[s - 1][1])
-            u = s + LEAD
-            if u < len(late):
-                grouped[u] = transpose_unit(late[u][0])
-            if 0 <= u - 1 < len(late):
-                quantise(grouped[u - 1], late[u - 1][1], late[u - 1][2])
-                if late[u - 1][1] is x_mx:
-                    rates[late[u - 1][2]] = first_product(late[u - 1][2])
-            if 0 <= u - 2 < len(late) and late[u - 2][1] is x_mx:
-                quantise_rates(rates[late[u - 2][2]], late[u - 2][2])
-            if 0 <= s + AHEAD < len(steps) and steps[s + AHEAD][0] >= GROUP:
-                difference_on_tensor(steps[s + AHEAD][0], steps[s + AHEAD][1])
+        def prepare(unit, shared=False):
+            grouped[unit] = transpose_unit(unit_of(unit[0], unit[1])[0], shared)
+
+        def finish(unit):
+            src, mx, i = unit_of(unit[0], unit[1])
+            quantise(grouped[unit], mx, i)
+
+        for s in range(4):
+            new_error(s)
+        early = [("x", 0), ("x", 1), ("w1", 0), ("w1", 1), ("w1", 2), ("w1", 3), ("som", 0), ("w2", 0), ("w3", 0)]
+        firsts = [psum_inh.tile([P, 4, P], F32, tag="inh", name="early_first") for j in range(PAIR)]
+        for n, unit in enumerate(early):
+            prepare(unit, n in (7, 8))
+            if 4 <= n < 8:
+                for j in range(PAIR):
+                    first_part(firsts[j], j, n - 4)
+            if n == 7:
+                for j in range(PAIR):
+                    rates[j] = rates_of(firsts[j])
+            if n >= 1:
+                finish(early[n - 1])
+        for j in range(PAIR):
+            quantise_rates(rates[j], j)
+
+        first = {}
+        for c in range(1, 4):
+            prepare(("w2", c))
+            prepare(("w3", c))
+            if c == 1:
+                finish(early[-1])
+                for s in range(2):
+                    difference_wide(s)
+                for s in range(2, 4):
+                    difference(s, 0, nc.gpsimd)
+            else:
+                finish(("w2", c - 1))
+                finish(("w3", c - 1))
+            if c == 2:
+                for s in range(2, 4):
+                    difference(s, 1, nc.vector)
+            for j in range(PAIR):
+                products(2 * ((c - 1) // 2) + j, ((c - 1) % 2,))
+            if c >= 2:
+                for j in range(PAIR):
+                    subtract(2 * ((c - 2) // 2) + j, ((c - 2) % 2,))
+        load_next()
+        relu(0)
+        finish(("w2", 3))
+        prepare(("x", 2))
+        finish(("w3", 3))
+        relu(1)
+        for j in range(PAIR):
+            products(2 + j, (1,))
+        for j in range(PAIR):
+            subtract(2 + j, (0,))
+        load_next()
+        finish(("x", 2))
+        prepare(("x", 3))
+        for j in range(PAIR):
+            subtract(2 + j, (1,))
+        first[2] = first_product(2)
+        relu(2)
+        rates[2] = rates_of(first[2])
+        filter_and_store(0)
+        finish(("x", 3))
+        filter_and_store(1)
+        quantise_rates(rates[2], 2)
+        for s in (4, 5):
+            new_error(s)
+            difference(s, 0, nc.gpsimd)
+            difference_on_tensor(s, 1)
+            if s == 4:
+                first[3] = first_product(3)
+                relu(3)
+                rates[3] = rates_of(first[3])
+        products(4)
+        load_next()
+        filter_and_store(2)
+        late = {4: [("x", 4), ("som", 1)], 5: [("x", 5)], 7: [("x", 6)], 9: [("x", 7)]}
+        for s in range(4, len(steps) + LAG):
+            load_next()
+            if s == 4:
+                quantise_rates(rates[3], 3)
+            if 5 <= s <= len(steps):
+                relu(s - 1)
+            for unit in late.get(s - 2, []):
+                if unit[0] == "x":
+                    rates[unit[1]] = rates_of(first[unit[1]])
+            if s >= 6:
+                filter_and_store(s - LAG)
+            if s < len(steps):
+                subtract(s)
+            if s == 4:
+                filter_and_store(3)
+            for unit in late.get(s - 1, []):
+                finish(unit)
+            for unit in late.get(s - 2, []):
+                if unit[0] == "x":
+                    quantise_rates(rates[unit[1]], unit[1])
+            for unit in late.get(s, []):
+                prepare(unit)
+            if s + 1 < len(steps):
+                products(s + 1)
+            n = s + 2
+            if n < len(steps):
+                new_error(n)
+                difference(n, 0, nc.gpsimd)
+                difference_on_tensor(n, 1)
+            for unit in late.get(s - 1, []):
+                if unit[0] == "x":
+                    first[unit[1]] = first_product(unit[1])

@@ -29,6 +29,7 @@ FLOPS = 2 * BATCH * D * NP * 3
 SLOTS = 4
 RES = 6
 LDS = 13
+FINE = 2
 LAG = 2
 
 
@@ -175,6 +176,9 @@ def tile_pecircuits_pb_kernel(
         banks = {}
         errs = {}
 
+        def pieces(s):
+            return [(0, CHUNK), (CHUNK, HALF)] if s >= len(steps) - FINE else [(0, HALF)]
+
         def new_error(s):
             errs[s] = errors.tile([P, HALF], F32, name="err")
 
@@ -225,17 +229,20 @@ def tile_pecircuits_pb_kernel(
                 )
 
         def relu(s):
-            nc.scalar.activation(out=errs[s][:], in_=errs[s][:], func=ACT.Relu, scale=0.1)
+            for lo, hi in pieces(s):
+                piece = errs[s][:, lo:hi]
+                nc.scalar.activation(out=piece, in_=piece, func=ACT.Relu, scale=0.1)
 
         def filter_and_store(s):
             j, h = steps[s]
-            cols = slice(h * HALF, (h + 1) * HALF)
             res = results.tile([P, HALF], F32, name="res")
-            nc.vector.scalar_tensor_tensor(
-                out=res[:], in0=half_of(rneg_raw[j // PAIR], j % PAIR)[:, cols], scalar=0.9, in1=errs[s][:],
-                op0=ALU.mult, op1=ALU.add,
-            )
-            nc.sync.dma_start(out=out_rows[:, j, cols], in_=res[:])
+            for lo, hi in pieces(s):
+                cols = slice(h * HALF + lo, h * HALF + hi)
+                nc.vector.scalar_tensor_tensor(
+                    out=res[:, lo:hi], in0=half_of(rneg_raw[j // PAIR], j % PAIR)[:, cols], scalar=0.9,
+                    in1=errs[s][:, lo:hi], op0=ALU.mult, op1=ALU.add,
+                )
+                nc.sync.dma_start(out=out_rows[:, j, cols], in_=res[:, lo:hi])
 
         def unit_of(name, i):
             if name == "x":
@@ -260,16 +267,28 @@ def tile_pecircuits_pb_kernel(
             new_error(s)
         early = [("x", 0), ("x", 1), ("w1", 0), ("w1", 1), ("w1", 2), ("w1", 3), ("som", 0), ("w2", 0), ("w3", 0)]
         firsts = [psum_inh.tile([P, 4, P], F32, tag="inh", name="early_first") for j in range(PAIR)]
+        def warm(count):
+            for i in range(count):
+                nc.tensor.matmul(out=warm_bank[:], lhsT=plus[:], rhs=zeros[:], start=True, stop=True)
+
+        warm_bank = psum_inh.tile([P, CHUNK], F32, tag="inh", name="warm_bank")
+        zeros = const.tile([P, CHUNK], BF16, name="zeros")
+        nc.vector.memset(zeros[:], 0.0)
+        warm(4)
         for n, unit in enumerate(early):
-            prepare(unit, n in (7, 8))
+            if n == 2:
+                warm(2)
+            if n in (3, 4):
+                warm(1)
+            prepare(unit, n in (99,))
+            if n >= 1 and n - 1 < 8:
+                finish(early[n - 1])
             if 4 <= n < 8:
                 for j in range(PAIR):
                     first_part(firsts[j], j, n - 4)
             if n == 7:
                 for j in range(PAIR):
                     rates[j] = rates_of(firsts[j])
-            if n >= 1:
-                finish(early[n - 1])
         for j in range(PAIR):
             quantise_rates(rates[j], j)
 

@@ -85,8 +85,8 @@ def tile_pecircuits_pb_kernel(
         som_rows = r_som.rearrange("(p j) k -> p (j k)", j=TILES)
         som_raw = loads.tile([P, 2 * UNIT], BF16, tag="raw", name="som_raw")
         nc.sync.dma_start(out=half_of(som_raw, 0), in_=half_of(som_rows, 0))
-        w23_raw[0] = load(w2_rows[0], w3_rows[0])
         pred_raw[0] = load(pair_of(pred_rows, 0))
+        w23_raw[0] = load(w2_rows[0], w3_rows[0])
         for c in range(1, CHUNKS):
             w23_raw[c] = load(w2_rows[c], w3_rows[c])
         x_raw[1] = load(pair_of(x_rows, 1))
@@ -283,6 +283,9 @@ def tile_pecircuits_pb_kernel(
             prepare(unit, n in (99,))
             if n >= 1 and n - 1 < 8:
                 finish(early[n - 1])
+            if n == 6:
+                difference_wide(0)
+                difference_wide(1)
             if 4 <= n < 8:
                 for j in range(PAIR):
                     first_part(firsts[j], j, n - 4)
@@ -298,8 +301,6 @@ def tile_pecircuits_pb_kernel(
             prepare(("w3", c))
             if c == 1:
                 finish(early[-1])
-                for s in range(2):
-                    difference_wide(s)
                 for s in range(2, 4):
                     difference(s, 0, nc.gpsimd)
             else:
@@ -346,24 +347,22 @@ def tile_pecircuits_pb_kernel(
         products(4)
         load_next()
         filter_and_store(2)
-        late = {4: [("x", 4), ("som", 1)], 5: [("x", 5)], 7: [("x", 6)], 9: [("x", 7)]}
+        late = {4: [("x", 4)], 5: [("som", 1)], 6: [("x", 5)], 8: [("x", 6)], 10: [("x", 7)]}
         for s in range(4, len(steps) + LAG):
             load_next()
             if s == 4:
                 quantise_rates(rates[3], 3)
-            if 5 <= s <= len(steps):
-                relu(s - 1)
             for unit in late.get(s - 2, []):
                 if unit[0] == "x":
                     rates[unit[1]] = rates_of(first[unit[1]])
             if s >= 6:
                 filter_and_store(s - LAG)
+            for unit in late.get(s - 1, []):
+                finish(unit)
             if s < len(steps):
                 subtract(s)
             if s == 4:
                 filter_and_store(3)
-            for unit in late.get(s - 1, []):
-                finish(unit)
             for unit in late.get(s - 2, []):
                 if unit[0] == "x":
                     quantise_rates(rates[unit[1]], unit[1])
@@ -371,6 +370,8 @@ def tile_pecircuits_pb_kernel(
                 prepare(unit)
             if s + 1 < len(steps):
                 products(s + 1)
+            if s < len(steps):
+                relu(s)
             n = s + 2
             if n < len(steps):
                 new_error(n)

@@ -27,9 +27,10 @@ HALF = D // 2
 FLOPS = 2 * BATCH * D * NP * 3
 
 SLOTS = 4
-RES = 6
+RES = 4
 LDS = 13
 FINE = 2
+SINGLE = 2
 LAG = 2
 
 
@@ -175,6 +176,7 @@ def tile_pecircuits_pb_kernel(
         steps = [(j, h) for h in range(2) for j in range(PAIR)] + [(j, h) for j in range(PAIR, TILES) for h in range(2)]
         banks = {}
         errs = {}
+        filtered = {}
 
         def pieces(s):
             return [(0, CHUNK), (CHUNK, HALF)] if s >= len(steps) - FINE else [(0, HALF)]
@@ -235,14 +237,19 @@ def tile_pecircuits_pb_kernel(
 
         def filter_and_store(s):
             j, h = steps[s]
-            res = results.tile([P, HALF], F32, name="res")
+            if h == 0:
+                filtered[j] = results.tile([P, D], F32, name="res")
+            res = filtered[j]
             for lo, hi in pieces(s):
                 cols = slice(h * HALF + lo, h * HALF + hi)
                 nc.vector.scalar_tensor_tensor(
-                    out=res[:, lo:hi], in0=half_of(rneg_raw[j // PAIR], j % PAIR)[:, cols], scalar=0.9,
+                    out=res[:, cols], in0=half_of(rneg_raw[j // PAIR], j % PAIR)[:, cols], scalar=0.9,
                     in1=errs[s][:, lo:hi], op0=ALU.mult, op1=ALU.add,
                 )
-                nc.sync.dma_start(out=out_rows[:, j, cols], in_=res[:, lo:hi])
+                if j >= TILES - SINGLE:
+                    nc.sync.dma_start(out=out_rows[:, j, cols], in_=res[:, cols])
+            if h == 1 and j < TILES - SINGLE:
+                nc.sync.dma_start(out=out_rows[:, j, :], in_=res[:])
 
         def unit_of(name, i):
             if name == "x":

@@ -305,47 +305,51 @@ def tile_pecircuits_pb_kernel(
         first = {}
         for c in range(1, 4):
             prepare(("w2", c))
+            if c == 3 and 0:
+                relu(0)
             prepare(("w3", c))
             if c == 1:
                 finish(early[-1])
-                for s in range(2, 4):
-                    difference(s, 0, nc.gpsimd)
             else:
                 finish(("w2", c - 1))
                 finish(("w3", c - 1))
             if c == 2:
                 for s in range(2, 4):
+                    difference(s, 0, nc.gpsimd)
                     difference(s, 1, nc.vector)
+
             for j in range(PAIR):
                 products(2 * ((c - 1) // 2) + j, ((c - 1) % 2,))
             if c >= 2:
                 for j in range(PAIR):
                     subtract(2 * ((c - 2) // 2) + j, ((c - 2) % 2,))
         load_next()
-        relu(0)
+        if not 0:
+            relu(0)
         finish(("w2", 3))
         prepare(("x", 2))
         finish(("w3", 3))
         relu(1)
         for j in range(PAIR):
             products(2 + j, (1,))
+
         for j in range(PAIR):
             subtract(2 + j, (0,))
         load_next()
         finish(("x", 2))
         prepare(("x", 3))
+        filter_and_store(0)
         for j in range(PAIR):
             subtract(2 + j, (1,))
         first[2] = first_product(2)
         relu(2)
         rates[2] = rates_of(first[2])
-        filter_and_store(0)
         finish(("x", 3))
         filter_and_store(1)
         quantise_rates(rates[2], 2)
         for s in (4, 5):
             new_error(s)
-            difference(s, 0, nc.gpsimd)
+            difference(s, 0, nc.gpsimd if s == 4 else nc.vector)
             difference_on_tensor(s, 1)
             if s == 4:
                 first[3] = first_product(3)

from contextlib import ExitStack

import concourse.mybir as mybir
from concourse.masks import make_identity

F32 = mybir.dt.float32
BF16 = mybir.dt.bfloat16
U32 = mybir.dt.uint32
U8 = mybir.dt.uint8
FP8X4 = mybir.dt.float8_e4m3fn_x4
ALU = mybir.AluOpType
ACT = mybir.ActivationFunctionType

P = 128
BATCH = 1024
D = 2048
NP = 512
TILES = BATCH // P
PAIR = 2
GROUP = 4
UNIT = 2048
WORDS = UNIT // 4
CHUNK = 512
CHUNKS = D // CHUNK
HALF = D // 2

FLOPS = 2 * BATCH * D * NP * 3

SLOTS = 4
RES = 4
LDS = 13
FINE = 2
SINGLE = 2
LAG = 2


def tile_pecircuits_pb_kernel(
    tc, x_batch, predicted, r_som, r_neg_batch, W_pv1_ff, W_inh_pe_neg, W_som_dend, out
):
    nc = tc.nc
    with ExitStack() as ctx:
        const = ctx.enter_context(tc.tile_pool(name="const", bufs=1))
        loads = ctx.enter_context(tc.tile_pool(name="loads", bufs=LDS))
        keep = ctx.enter_context(tc.tile_pool(name="keep", bufs=1))
        stage = ctx.enter_context(tc.tile_pool(name="stage", bufs=4))
        errors = ctx.enter_context(tc.tile_pool(name="errors", bufs=SLOTS))
        results = ctx.enter_context(tc.tile_pool(name="results", bufs=RES))
        psum_prep = ctx.enter_context(tc.psum_pool(name="psum_prep", bufs=4))
        psum_inh = ctx.enter_context(tc.psum_pool(name="psum_inh", bufs=4))
        ctx.enter_context(tc.manual_schedule())

        ident = const.tile([P, P], F32)
        make_identity(nc, ident[:])
        plus = const.tile([P, P], BF16)
        make_identity(nc, plus[:])
        minus = const.tile([P, P], BF16)
        nc.gpsimd.tensor_scalar_mul(out=minus[:], in0=plus[:], scalar1=-1.0)

        def load(*views):
            raw = loads.tile([P, 2 * UNIT], BF16, tag="raw", name="raw")
            width = 2 * UNIT // len(views)
            for i, view in enumerate(views):
                nc.sync.dma_start(out=raw[:, i * width : (i + 1) * width], in_=view)
            return raw

        def half_of(raw, i):
            return raw[:, i * UNIT : (i + 1) * UNIT]

        x_rows = x_batch.rearrange("(p j) d -> p (j d)", j=TILES)
        pred_rows = predicted.rearrange("(p j) d -> p (j d)", j=TILES)
        rneg_rows = r_neg_batch.rearrange("(p j) d -> p (j d)", j=TILES)
        out_rows = out.rearrange("(p j) d -> p j d", j=TILES)
        w1_rows = W_pv1_ff.rearrange("(u p e) k -> u p (e k)", u=2, e=2)
        w2_rows = W_inh_pe_neg.rearrange("(c p t) k -> c p (t k)", c=CHUNKS, t=4)
        w3_rows = W_som_dend.rearrange("(c p t) k -> c p (t k)", c=CHUNKS, t=4)

        def pair_of(rows, q):
            return rows[:, q * PAIR * D : (q + 1) * PAIR * D]

        def tile_of(rows, j):
            return rows[:, j * D : (j + 1) * D]

        x_raw, pred_raw, rneg_raw, w23_raw = {}, {}, {}, {}
        x_raw[0] = load(tile_of(x_rows, 0), tile_of(x_rows, 1))
        w1_raw = [load(w1_rows[u]) for u in range(2)]
        som_rows = r_som.rearrange("(p j) k -> p (j k)", j=TILES)
        som_raw = loads.tile([P, 2 * UNIT], BF16, tag="raw", name="som_raw")
        nc.sync.dma_start(out=half_of(som_raw, 0), in_=half_of(som_rows, 0))
        pred_raw[0] = load(pair_of(pred_rows, 0))
        w23_raw[0] = load(w2_rows[0], w3_rows[0])
        for c in range(1, CHUNKS):
            w23_raw[c] = load(w2_rows[c], w3_rows[c])
        x_raw[1] = load(pair_of(x_rows, 1))
        rneg_raw[0] = load(pair_of(rneg_rows, 0))
        pred_raw[1] = load(pair_of(pred_rows, 1))
        nc.sync.dma_start(out=half_of(som_raw, 1), in_=half_of(som_rows, 1))
        pending = [(x_raw, x_rows, 2), (rneg_raw, rneg_rows, 1), (pred_raw, pred_rows, 2), (x_raw, x_rows, 3), (rneg_raw, rneg_rows, 2), (pred_raw, pred_rows, 3), (rneg_raw, rneg_rows, 3)]

        def load_next():
            if pending:
                raws, rows, q = pending.pop(0)
                raws[q] = load(pair_of(rows, q))

        def mx_tiles(units, name):
            codes = keep.tile([P, units, WORDS], U32, align_bytes=64, name=name + "_codes")
            scales = keep.tile([P, units, WORDS], U8, align_bytes=64, name=name + "_scales")
            return codes, scales

        x_mx = mx_tiles(TILES, "x")
        w1_mx = mx_tiles(4, "w1")
        w2_mx = mx_tiles(CHUNKS, "w2")
        w3_mx = mx_tiles(CHUNKS, "w3")
        som_mx = mx_tiles(2, "som")
        r_mx = mx_tiles(2, "r")

        def transpose_half(src, grouped, half, on_vector):
            words = src.bitcast(F32)
            grouped_words = grouped[:].bitcast(F32).rearrange("p (a r h) -> p a r h", a=4, h=2)
            bank = psum_prep.tile([P, 2, 2, P], F32, tag="prep", name="bank")
            for a in range(2):
                for h in range(2):
                    start = (4 * half + 2 * a + h) * P
                    nc.tensor.transpose(bank[:, a, h, :], words[:, start : start + P], ident[:])
            copy = nc.vector.tensor_copy if on_vector else nc.scalar.copy
            copy(
                out=grouped_words[:, 2 * half : 2 * half + 2, :, :],
                in_=bank[:].rearrange("p a h r -> p a r h"),
            )

        def transpose_unit(src, shared=False):
            grouped = stage.tile([P, UNIT], BF16, align_bytes=64, name="grouped")
            for half in range(2):
                transpose_half(src, grouped, half, shared and half == 1)
            return grouped

        def quantise(grouped, mx, unit):
            nc.vector.quantize_mx(out=mx[0][:, unit, :].bitcast(FP8X4), scales=mx[1][:, unit, :], in_=grouped[:])

        def x_tile(j):
            return half_of(x_raw[j // PAIR], j % PAIR)

        def pred_tile(j):
            return half_of(pred_raw[j // PAIR], j % PAIR)

        def operand(mx, unit, cols):
            return mx[0][:, unit, cols].bitcast(FP8X4), mx[1][:, unit, cols]

        def batch_operand(mx, j):
            return operand(mx, j // 4, slice((j % 4) * P, (j % 4 + 1) * P))

        def first_part(first, j, t):
                for g in range(4):
                    k_cols = slice(g * P, (g + 1) * P)
                    w_codes, w_scales = operand(w1_mx, t, k_cols)
                    b_codes, b_scales = operand(x_mx, j, k_cols)
                    nc.tensor.matmul_mx(
                        out=first[:, t, :], lhsT=w_codes, lhsT_scale=w_scales, rhs=b_codes, rhs_scale=b_scales,
                        start=(g == 0), stop=(g == 3),
                    )

        def rates_of(first):
            rates = stage.tile([P, P, 4], BF16, align_bytes=64, name="rates")
            nc.scalar.activation(out=rates[:], in_=first[:].rearrange("p t r -> p r t"), func=ACT.Relu)
            return rates

        def first_product(j):
            first = psum_prep.tile([P, 4, P], F32, tag="prep", name="first")
            for t in range(4):
                first_part(first, j, t)
            return first

        def quantise_rates(rates, j):
            codes, scales = batch_operand(r_mx, j)
            nc.vector.quantize_mx(out=codes, scales=scales, in_=rates[:].rearrange("p r t -> p (r t)"))

        steps = [(j, h) for h in range(2) for j in range(PAIR)] + [(j, h) for j in range(PAIR, TILES) for h in range(2)]
        banks = {}
        errs = {}
        filtered = {}

        def pieces(s):
            return [(0, CHUNK), (CHUNK, HALF)] if s >= len(steps) - FINE else [(0, HALF)]

        def new_error(s):
            errs[s] = errors.tile([P, HALF], F32, name="err")

        def difference(s, i, engine):
            j, h = steps[s]
            cols = slice((2 * h + i) * CHUNK, (2 * h + i + 1) * CHUNK)
            piece = errs[s][:, i * CHUNK : (i + 1) * CHUNK]
            engine.tensor_tensor(out=piece, in0=pred_tile(j)[:, cols], in1=x_tile(j)[:, cols], op=ALU.subtract)

        def difference_wide(s):
            j, h = steps[s]
            cols = slice(h * HALF, (h + 1) * HALF)
            nc.vector.tensor_tensor(out=errs[s][:], in0=pred_tile(j)[:, cols], in1=x_tile(j)[:, cols], op=ALU.subtract)

        def difference_on_tensor(s, i):
            j, h = steps[s]
            cols = slice((2 * h + i) * CHUNK, (2 * h + i + 1) * CHUNK)
            piece = errs[s][:, i * CHUNK : (i + 1) * CHUNK]
            diff = psum_prep.tile([P, CHUNK], F32, tag="prep", name="diff")
            nc.tensor.matmul(out=diff[:], lhsT=plus[:], rhs=pred_tile(j)[:, cols], start=True, stop=False)
            nc.tensor.matmul(out=diff[:], lhsT=minus[:], rhs=x_tile(j)[:, cols], start=False, stop=True)
            nc.scalar.copy(out=piece, in_=diff[:])

        def products(s, which=(0, 1)):
            j, h = steps[s]
            r_codes, r_scales = batch_operand(r_mx, j)
            s_codes, s_scales = batch_operand(som_mx, j)
            banks.setdefault(s, [])
            for c in (2 * h + i for i in which):
                w2_codes, w2_scales = operand(w2_mx, c, slice(0, WORDS))
                w3_codes, w3_scales = operand(w3_mx, c, slice(0, WORDS))
                inh = psum_inh.tile([P, CHUNK], F32, tag="inh", name="inh")
                nc.tensor.matmul_mx(
                    out=inh[:], lhsT=r_codes, lhsT_scale=r_scales, rhs=w2_codes, rhs_scale=w2_scales,
                    start=True, stop=False,
                )
                nc.tensor.matmul_mx(
                    out=inh[:], lhsT=s_codes, lhsT_scale=s_scales, rhs=w3_codes, rhs_scale=w3_scales,
                    start=False, stop=True,
                )
                banks[s].append(inh)

        def subtract(s, which=(0, 1)):
            for i in which:
                piece = errs[s][:, i * CHUNK : (i + 1) * CHUNK].rearrange("p (r t) -> p r t", t=4)
                nc.vector.tensor_tensor(
                    out=piece, in0=piece, in1=banks[s][i][:].rearrange("p (t r) -> p r t", t=4), op=ALU.subtract
                )

        def relu(s):
            for lo, hi in pieces(s):
                piece = errs[s][:, lo:hi]
                nc.scalar.activation(out=piece, in_=piece, func=ACT.Relu, scale=0.1)

        def filter_and_store(s):
            j, h = steps[s]
            if h == 0:
                filtered[j] = results.tile([P, D], F32, name="res")
            res = filtered[j]
            for lo, hi in pieces(s):
                cols = slice(h * HALF + lo, h * HALF + hi)
                nc.vector.scalar_tensor_tensor(
                    out=res[:, cols], in0=half_of(rneg_raw[j // PAIR], j % PAIR)[:, cols], scalar=0.9,
                    in1=errs[s][:, lo:hi], op0=ALU.mult, op1=ALU.add,
                )
                if j >= TILES - SINGLE:
                    nc.sync.dma_start(out=out_rows[:, j, cols], in_=res[:, cols])
            if h == 1 and j < TILES - SINGLE:
                nc.sync.dma_start(out=out_rows[:, j, :], in_=res[:])

        def unit_of(name, i):
            if name == "x":
                return x_tile(i), x_mx, i
            if name == "w1":
                return half_of(w1_raw[i // 2], i % 2), w1_mx, i
            if name == "som":
                return half_of(som_raw, i), som_mx, i
            return half_of(w23_raw[i], 0 if name == "w2" else 1), (w2_mx if name == "w2" else w3_mx), i

        rates = {}
        grouped = {}

        def prepare(unit, shared=False):
            grouped[unit] = transpose_unit(unit_of(unit[0], unit[1])[0], shared)

        def finish(unit):
            src, mx, i = unit_of(unit[0], unit[1])
            quantise(grouped[unit], mx, i)

        for s in range(4):
            new_error(s)
        early = [("x", 0), ("x", 1), ("w1", 0), ("w1", 1), ("w1", 2), ("w1", 3), ("som", 0), ("w2", 0), ("w3", 0)]
        firsts = [psum_inh.tile([P, 4, P], F32, tag="inh", name="early_first") for j in range(PAIR)]
        def warm(count):
            for i in range(count):
                nc.tensor.matmul(out=warm_bank[:], lhsT=plus[:], rhs=zeros[:], start=True, stop=True)

        warm_bank = psum_inh.tile([P, CHUNK], F32, tag="inh", name="warm_bank")
        zeros = const.tile([P, CHUNK], BF16, name="zeros")
        nc.vector.memset(zeros[:], 0.0)
        warm(4)
        for n, unit in enumerate(early):
            if n == 2:
                warm(2)
            if n in (3, 4):
                warm(1)
            prepare(unit, n in (99,))
            if n >= 1 and n - 1 < 8:
                finish(early[n - 1])
            if n == 6:
                difference_wide(0)
                difference_wide(1)
            if 4 <= n < 8:
                for j in range(PAIR):
                    first_part(firsts[j], j, n - 4)
            if n == 7:
                for j in range(PAIR):
                    rates[j] = rates_of(firsts[j])
        for j in range(PAIR):
            quantise_rates(rates[j], j)

        first = {}
        for c in range(1, 4):
            prepare(("w2", c))
            if c == 3 and 0:
                relu(0)
            prepare(("w3", c))
            if c == 1:
                finish(early[-1])
            else:
                finish(("w2", c - 1))
                finish(("w3", c - 1))
            if c == 2:
                for s in range(2, 4):
                    difference(s, 0, nc.gpsimd)
                    difference(s, 1, nc.vector)

            for j in range(PAIR):
                products(2 * ((c - 1) // 2) + j, ((c - 1) % 2,))
            if c >= 2:
                for j in range(PAIR):
                    subtract(2 * ((c - 2) // 2) + j, ((c - 2) % 2,))
        load_next()
        if not 0:
            relu(0)
        finish(("w2", 3))
        prepare(("x", 2))
        finish(("w3", 3))
        relu(1)
        for j in range(PAIR):
            products(2 + j, (1,))

        for j in range(PAIR):
            subtract(2 + j, (0,))
        load_next()
        finish(("x", 2))
        prepare(("x", 3))
        filter_and_store(0)
        for j in range(PAIR):
            subtract(2 + j, (1,))
        first[2] = first_product(2)
        relu(2)
        rates[2] = rates_of(first[2])
        finish(("x", 3))
        filter_and_store(1)
        quantise_rates(rates[2], 2)
        for s in (4, 5):
            new_error(s)
            difference(s, 0, nc.gpsimd if s == 4 else nc.vector)
            difference_on_tensor(s, 1)
            if s == 4:
                first[3] = first_product(3)
                relu(3)
                rates[3] = rates_of(first[3])
        products(4)
        load_next()
        filter_and_store(2)
        late = {4: [("x", 4)], 5: [("som", 1)], 6: [("x", 5)], 8: [("x", 6)], 10: [("x", 7)]}
        for s in range(4, len(steps) + LAG):
            load_next()
            if s == 4:
                quantise_rates(rates[3], 3)
            for unit in late.get(s - 2, []):
                if unit[0] == "x":
                    rates[unit[1]] = rates_of(first[unit[1]])
            if s >= 6:
                filter_and_store(s - LAG)
            for unit in late.get(s - 1, []):
                finish(unit)
            if s < len(steps):
                subtract(s)
            if s == 4:
                filter_and_store(3)
            for unit in late.get(s - 2, []):
                if unit[0] == "x":
                    quantise_rates(rates[unit[1]], unit[1])
            for unit in late.get(s, []):
                prepare(unit)
            if s + 1 < len(steps):
                products(s + 1)
            if s < len(steps):
                relu(s)
            n = s + 2
            if n < len(steps):
                new_error(n)
                difference(n, 0, nc.gpsimd)
                difference_on_tensor(n, 1)
            for unit in late.get(s - 1, []):
                if unit[0] == "x":
                    first[unit[1]] = first_product(unit[1])
